import numpy as np
import ml_dtypes


def mxq(x, axis, fmt="e4m3"):
    dtype, down = {"e4m3": (ml_dtypes.float8_e4m3fn, 7), "e5m2": (ml_dtypes.float8_e5m2, 14)}[fmt]
    v = np.moveaxis(np.asarray(x, np.float32).astype(ml_dtypes.bfloat16).astype(np.float64), axis, -1)
    blocks = v.reshape(v.shape[:-1] + (-1, 32))
    amax = np.abs(blocks).max(-1, keepdims=True)
    byte = np.maximum(np.where(amax > 0, np.frexp(amax)[1] - 1 + 127, 0) - down, 1)
    scale = np.exp2(byte - 127.0)
    codes = (blocks / scale).astype(np.float32).astype(dtype).astype(np.float64)
    return np.moveaxis((codes * scale).reshape(v.shape), -1, axis)


WIDE = False


def mx_kscale(k):
    if not WIDE:
        return np.ones(k)
    levels = np.array([10, -10, 5, -5, 0])
    a = np.random.permutation(np.resize(levels, k // 512 * 4)).reshape(k // 512, 4)
    idx = np.arange(k)
    return np.exp2(a[idx // 512, idx % 128 // 32])


BF16 = ml_dtypes.bfloat16


def bf(x):
    return np.asarray(x, np.float32).astype(BF16)


def f64(x):
    return np.asarray(x).astype(np.float64)


E2M1 = np.array([0.0, 0.5, 1.0, 1.5, 2.0, 3.0, 4.0, 6.0, -0.0, -0.5, -1.0, -1.5, -2.0, -3.0, -4.0, -6.0])


def pack_weight(w, fmt):
    k, n = w.shape
    w = f64(bf(w)).reshape(k // 32, 32, n)
    amax = np.abs(w).max(1)
    if fmt == "e4m3":
        byte = np.frexp(amax)[1] - 1 + 127 - 7
    else:
        mant, ex = np.frexp(amax / 6.0)
        byte = np.where(mant > 0.5, ex, ex - 1) + 127
    byte = np.clip(np.where(amax > 0, byte, 1), 1, 254)
    scaled = (w * np.exp2(127.0 - byte)[:, None, :]).reshape(k, n).astype(np.float32)
    by_word = np.ascontiguousarray(scaled.reshape(k // 512, 128, 4, n).transpose(0, 1, 3, 2))
    if fmt == "e4m3":
        words = by_word.astype(ml_dtypes.float8_e4m3fn).view(np.uint8)
    else:
        c = by_word.astype(ml_dtypes.float4_e2m1fn).view(np.uint8) & 0xF
        words = c[..., 0::2] | (c[..., 1::2] << 4)
    return np.ascontiguousarray(words), np.ascontiguousarray(byte.astype(np.uint8).reshape(k // 512, 16, n))


def unpack_weight(words, scales, fmt):
    g, p, n, _ = words.shape
    if fmt == "e4m3":
        vals = np.ascontiguousarray(words).view(ml_dtypes.float8_e4m3fn).astype(np.float64)
    else:
        nib = np.empty((g, p, n, 4), np.uint8)
        nib[..., 0::2] = words & 0xF
        nib[..., 1::2] = words >> 4
        vals = E2M1[nib]
    vals = vals * np.repeat(np.exp2(scales.astype(np.float64) - 127.0), 8, axis=1)[..., None]
    return vals.transpose(0, 1, 3, 2).reshape(g * 512, n)


B, CIN, COUT, H, W = 4, 512, 512, 32, 32


def setup_inputs():
    s = mx_kscale(CIN)
    x = np.random.standard_normal((B, CIN, H, W)) * s[None, :, None, None]
    weight = np.random.uniform(-1.0, 1.0, (CIN, COUT)) * np.sqrt(3.0 / CIN) / s[:, None]
    words, scales = pack_weight(weight, "e4m3")
    return {"x": bf(x), "weight_words": words, "weight_scales": scales}


def reference(x, weight_words, weight_scales):
    wq = unpack_weight(weight_words, weight_scales, "e4m3")
    xq = mxq(f64(x), 1, "e4m3")
    return np.einsum("io,bihw->bohw", wq, xq, optimize=True)

@@ -1,0 +1,100 @@
+from contextlib import ExitStack
+
+import concourse.mybir as mybir
+
+FP8X4 = mybir.dt.float8_e4m3fn_x4
+BF16 = mybir.dt.bfloat16
+F32 = mybir.dt.float32
+I32 = mybir.dt.int32
+U32 = mybir.dt.uint32
+U8 = mybir.dt.uint8
+
+P = 128
+PACK = 4
+IMAGES = 4
+C_IN = P * PACK
+C_OUT = 512
+PIXELS = 32 * 32
+O_TILE = 128
+PX_TILE = 512
+O_TILES = C_OUT // O_TILE
+PX_TILES = PIXELS // PX_TILE
+PSUM_BANKS = 8
+RUN = 4
+
+FLOPS = 2 * IMAGES * PIXELS * C_IN * C_OUT
+
+
+def load_image(nc, pool, x, b):
+    raw = pool.tile([P, PACK, PIXELS], BF16)
+    nc.sync.dma_start(out=raw[:], in_=x[b].rearrange("(p j) h w -> p j (h w)", j=PACK))
+    return raw
+
+
+def load_weight(nc, pool, weight_words, weight_scales):
+    w_codes = pool.tile([P, C_OUT], U32, align_bytes=64)
+    nc.sync.dma_start(
+        out=w_codes[:].bitcast(I32),
+        in_=weight_words[0].rearrange("p n t -> p (n t)").bitcast(I32),
+    )
+    w_scales = pool.tile([P, C_OUT], U8, align_bytes=64)
+    nc.vector.memset(w_scales[:].bitcast(I32), 0)
+    for quadrant in range(4):
+        nc.sync.dma_start(
+            out=w_scales[32 * quadrant : 32 * quadrant + 4, :].bitcast(I32),
+            in_=weight_scales[0, 4 * quadrant : 4 * quadrant + 4, :].bitcast(I32),
+        )
+    return w_codes, w_scales
+
+
+def tile_simpleconvolution_kernel(tc, x, weight_words, weight_scales, out):
+    nc = tc.nc
+    with ExitStack() as ctx:
+        weight_pool = ctx.enter_context(tc.tile_pool(name="weight", bufs=1))
+        image_pool = ctx.enter_context(tc.tile_pool(name="image", bufs=IMAGES))
+        result_pool = ctx.enter_context(tc.tile_pool(name="result", bufs=IMAGES * O_TILES))
+        psum = ctx.enter_context(tc.psum_pool(name="psum", bufs=PSUM_BANKS))
+
+        raws = [load_image(nc, image_pool, x, 0)]
+        w_codes, w_scales = load_weight(nc, weight_pool, weight_words, weight_scales)
+        for b in range(1, IMAGES):
+            raws.append(load_image(nc, image_pool, x, b))
+
+        for b in range(IMAGES):
+            raw = raws[b]
+            grouped = image_pool.tile([P, PIXELS, PACK], BF16, align_bytes=64)
+            x_codes = image_pool.tile([P, PIXELS], U32, align_bytes=64)
+            x_scales = image_pool.tile([P, PIXELS], U8, align_bytes=64)
+            px_slices = [slice(n * PX_TILE, (n + 1) * PX_TILE) for n in range(PX_TILES)]
+            for px in px_slices:
+                nc.vector.tensor_copy(
+                    out=grouped[:, px, :].rearrange("p (c i) j -> p c j i", i=RUN),
+                    in_=raw[:, :, px].rearrange("p j (c i) -> p c j i", i=RUN),
+                )
+            for px in px_slices:
+                nc.vector.quantize_mx(
+                    out=x_codes[:, px].bitcast(FP8X4),
+                    scales=x_scales[:, px],
+                    in_=grouped[:, px, :].rearrange("p w j -> p (w j)"),
+                )
+
+            out_b = out[b].rearrange("(m p) h w -> m p (h w)", p=O_TILE)
+            for m in range(O_TILES):
+                o_cols = slice(m * O_TILE, (m + 1) * O_TILE)
+                result = result_pool.tile([P, PIXELS], F32)
+                for n, px in enumerate(px_slices):
+                    acc = psum.tile([P, PX_TILE], F32)
+                    nc.tensor.matmul_mx(
+                        out=acc[:],
+                        lhsT=w_codes[:, o_cols].bitcast(FP8X4),
+                        lhsT_scale=w_scales[:, o_cols],
+                        rhs=x_codes[:, px].bitcast(FP8X4),
+                        rhs_scale=x_scales[:, px],
+                        start=True,
+                        stop=True,
+                    )
+                    if m == 0 and n == 0:
+                        nc.vector.tensor_copy(out=result[:, px], in_=acc[:])
+                    else:
+                        nc.scalar.copy(out=result[:, px], in_=acc[:])
+                nc.sync.dma_start(out=out_b[m], in_=result[:])

@@ -18,7 +18,8 @@ PIXELS = 32 * 32
 O_TILE = 128
 PX_TILE = 512
 O_TILES = C_OUT // O_TILE
-PX_TILES = PIXELS // PX_TILE
+HALVES = PIXELS // PX_TILE
+UNITS = IMAGES * HALVES
 PSUM_BANKS = 8
 RUN = 4
 
@@ -32,11 +33,6 @@ def load_image(nc, pool, x, b):
 
 
 def load_weight(nc, pool, weight_words, weight_scales):
-    w_codes = pool.tile([P, C_OUT], U32, align_bytes=64)
-    nc.sync.dma_start(
-        out=w_codes[:].bitcast(I32),
-        in_=weight_words[0].rearrange("p n t -> p (n t)").bitcast(I32),
-    )
     w_scales = pool.tile([P, C_OUT], U8, align_bytes=64)
     nc.vector.memset(w_scales[:].bitcast(I32), 0)
     for quadrant in range(4):
@@ -44,6 +40,11 @@ def load_weight(nc, pool, weight_words, weight_scales):
             out=w_scales[32 * quadrant : 32 * quadrant + 4, :].bitcast(I32),
             in_=weight_scales[0, 4 * quadrant : 4 * quadrant + 4, :].bitcast(I32),
         )
+    w_codes = pool.tile([P, C_OUT], U32, align_bytes=64)
+    nc.sync.dma_start(
+        out=w_codes[:].bitcast(I32),
+        in_=weight_words[0].rearrange("p n t -> p (n t)").bitcast(I32),
+    )
     return w_codes, w_scales
 
 
@@ -52,49 +53,70 @@ def tile_simpleconvolution_kernel(tc, x, weight_words, weight_scales, out):
     with ExitStack() as ctx:
         weight_pool = ctx.enter_context(tc.tile_pool(name="weight", bufs=1))
         image_pool = ctx.enter_context(tc.tile_pool(name="image", bufs=IMAGES))
+        unit_pool = ctx.enter_context(tc.tile_pool(name="unit", bufs=UNITS))
         result_pool = ctx.enter_context(tc.tile_pool(name="result", bufs=IMAGES * O_TILES))
         psum = ctx.enter_context(tc.psum_pool(name="psum", bufs=PSUM_BANKS))
+        ctx.enter_context(tc.manual_schedule())
 
         raws = [load_image(nc, image_pool, x, 0)]
         w_codes, w_scales = load_weight(nc, weight_pool, weight_words, weight_scales)
         for b in range(1, IMAGES):
             raws.append(load_image(nc, image_pool, x, b))
 
-        for b in range(IMAGES):
-            raw = raws[b]
-            grouped = image_pool.tile([P, PIXELS, PACK], BF16, align_bytes=64)
-            x_codes = image_pool.tile([P, PIXELS], U32, align_bytes=64)
-            x_scales = image_pool.tile([P, PIXELS], U8, align_bytes=64)
-            px_slices = [slice(n * PX_TILE, (n + 1) * PX_TILE) for n in range(PX_TILES)]
-            for px in px_slices:
-                nc.vector.tensor_copy(
-                    out=grouped[:, px, :].rearrange("p (c i) j -> p c j i", i=RUN),
-                    in_=raw[:, :, px].rearrange("p j (c i) -> p c j i", i=RUN),
-                )
-            for px in px_slices:
-                nc.vector.quantize_mx(
-                    out=x_codes[:, px].bitcast(FP8X4),
-                    scales=x_scales[:, px],
-                    in_=grouped[:, px, :].rearrange("p w j -> p (w j)"),
-                )
+        grouped = {}
+        x_codes = {}
+        x_scales = {}
 
+        def regroup(u, engine_copy):
+            b, n = divmod(u, HALVES)
+            px = slice(n * PX_TILE, (n + 1) * PX_TILE)
+            g = unit_pool.tile([P, PX_TILE, PACK], BF16, align_bytes=64, name="grouped")
+            engine_copy(
+                out=g[:].rearrange("p (c i) j -> p c j i", i=RUN),
+                in_=raws[b][:, :, px].rearrange("p j (c i) -> p c j i", i=RUN),
+            )
+            grouped[u] = g
+
+        def quantise(u):
+            codes = unit_pool.tile([P, PX_TILE], U32, align_bytes=64, name="codes")
+            scales = unit_pool.tile([P, PX_TILE], U8, align_bytes=64, name="scales")
+            nc.vector.quantize_mx(
+                out=codes[:].bitcast(FP8X4),
+                scales=scales[:],
+                in_=grouped[u][:].rearrange("p w j -> p (w j)"),
+            )
+            x_codes[u] = codes
+            x_scales[u] = scales
+
+        def multiply(u, m):
+            o_cols = slice(m * O_TILE, (m + 1) * O_TILE)
+            acc = psum.tile([P, PX_TILE], F32, name="acc")
+            nc.tensor.matmul_mx(
+                out=acc[:],
+                lhsT=w_codes[:, o_cols].bitcast(FP8X4),
+                lhsT_scale=w_scales[:, o_cols],
+                rhs=x_codes[u][:].bitcast(FP8X4),
+                rhs_scale=x_scales[u][:],
+                start=True,
+                stop=True,
+            )
+            return acc
+
+        on_vector = nc.vector.tensor_copy
+        on_scalar = nc.scalar.copy
+        vector_tiles = ((), (0,), (0,), (0, 2))
+
+        for b in range(IMAGES):
+            units = [HALVES * b + n for n in range(HALVES)]
+            regroup(units[0], on_vector)
+            regroup(units[1], on_scalar if b == 0 else on_vector)
+            for u in units:
+                quantise(u)
             out_b = out[b].rearrange("(m p) h w -> m p (h w)", p=O_TILE)
             for m in range(O_TILES):
-                o_cols = slice(m * O_TILE, (m + 1) * O_TILE)
-                result = result_pool.tile([P, PIXELS], F32)
-                for n, px in enumerate(px_slices):
-                    acc = psum.tile([P, PX_TILE], F32)
-                    nc.tensor.matmul_mx(
-                        out=acc[:],
-                        lhsT=w_codes[:, o_cols].bitcast(FP8X4),
-                        lhsT_scale=w_scales[:, o_cols],
-                        rhs=x_codes[:, px].bitcast(FP8X4),
-                        rhs_scale=x_scales[:, px],
-                        start=True,
-                        stop=True,
-                    )
-                    if m == 0 and n == 0:
-                        nc.vector.tensor_copy(out=result[:, px], in_=acc[:])
-                    else:
-                        nc.scalar.copy(out=result[:, px], in_=acc[:])
+                engine_copy = on_vector if m in vector_tiles[b] else on_scalar
+                result = result_pool.tile([P, PIXELS], F32, name="result")
+                for n, u in enumerate(units):
+                    acc = multiply(u, m)
+                    engine_copy(out=result[:, n * PX_TILE : (n + 1) * PX_TILE], in_=acc[:])
                 nc.sync.dma_start(out=out_b[m], in_=result[:])

@@ -54,7 +54,7 @@ def tile_simpleconvolution_kernel(tc, x, weight_words, weight_scales, out):
         weight_pool = ctx.enter_context(tc.tile_pool(name="weight", bufs=1))
         image_pool = ctx.enter_context(tc.tile_pool(name="image", bufs=IMAGES))
         unit_pool = ctx.enter_context(tc.tile_pool(name="unit", bufs=UNITS))
-        result_pool = ctx.enter_context(tc.tile_pool(name="result", bufs=IMAGES * O_TILES))
+        result_pool = ctx.enter_context(tc.tile_pool(name="result", bufs=9))
         psum = ctx.enter_context(tc.psum_pool(name="psum", bufs=PSUM_BANKS))
         ctx.enter_context(tc.manual_schedule())
 
@@ -105,6 +105,7 @@ def tile_simpleconvolution_kernel(tc, x, weight_words, weight_scales, out):
         on_vector = nc.vector.tensor_copy
         on_scalar = nc.scalar.copy
         vector_tiles = ((), (0,), (0,), (0, 2))
+        store_groups = (((0,), (1,), (2, 3)), ((0, 1), (2, 3)), ((0, 1), (2, 3)), ((0, 1), (2, 3)))
 
         for b in range(IMAGES):
             units = [HALVES * b + n for n in range(HALVES)]
@@ -112,11 +113,12 @@ def tile_simpleconvolution_kernel(tc, x, weight_words, weight_scales, out):
             regroup(units[1], on_scalar if b == 0 else on_vector)
             for u in units:
                 quantise(u)
-            out_b = out[b].rearrange("(m p) h w -> m p (h w)", p=O_TILE)
-            for m in range(O_TILES):
-                engine_copy = on_vector if m in vector_tiles[b] else on_scalar
-                result = result_pool.tile([P, PIXELS], F32, name="result")
-                for n, u in enumerate(units):
-                    acc = multiply(u, m)
-                    engine_copy(out=result[:, n * PX_TILE : (n + 1) * PX_TILE], in_=acc[:])
-                nc.sync.dma_start(out=out_b[m], in_=result[:])
+            out_b = out[b].rearrange("(m p) h w -> p m (h w)", p=O_TILE)
+            for group in store_groups[b]:
+                result = result_pool.tile([P, len(group), PIXELS], F32, name="result")
+                for i, m in enumerate(group):
+                    engine_copy = on_vector if m in vector_tiles[b] else on_scalar
+                    for n, u in enumerate(units):
+                        acc = multiply(u, m)
+                        engine_copy(out=result[:, i, n * PX_TILE : (n + 1) * PX_TILE], in_=acc[:])
+                nc.sync.dma_start(out=out_b[:, group[0] : group[-1] + 1, :], in_=result[:])

@@ -33,17 +33,32 @@ def load_image(nc, pool, x, b):
 
 
 def load_weight(nc, pool, weight_words, weight_scales):
-    w_scales = pool.tile([P, C_OUT], U8, align_bytes=64)
-    nc.vector.memset(w_scales[:].bitcast(I32), 0)
+    raw_scales = pool.tile([P, O_TILES, O_TILE], U8, align_bytes=64)
+    flat_scales = raw_scales[:].rearrange("p m q -> p (m q)")
+    nc.vector.memset(flat_scales.bitcast(I32), 0)
     for quadrant in range(4):
         nc.sync.dma_start(
-            out=w_scales[32 * quadrant : 32 * quadrant + 4, :].bitcast(I32),
+            out=flat_scales[32 * quadrant : 32 * quadrant + 4, :].bitcast(I32),
             in_=weight_scales[0, 4 * quadrant : 4 * quadrant + 4, :].bitcast(I32),
         )
-    w_codes = pool.tile([P, C_OUT], U32, align_bytes=64)
+    raw_codes = pool.tile([P, O_TILES, O_TILE], U32, align_bytes=64)
     nc.sync.dma_start(
-        out=w_codes[:].bitcast(I32),
+        out=raw_codes[:].rearrange("p m q -> p (m q)").bitcast(I32),
         in_=weight_words[0].rearrange("p n t -> p (n t)").bitcast(I32),
+    )
+    return raw_codes, raw_scales
+
+
+def permute_weight(nc, pool, raw_codes, raw_scales):
+    w_codes = pool.tile([P, O_TILES, O_TILE], U32, align_bytes=64)
+    nc.vector.tensor_copy(
+        out=w_codes[:].bitcast(I32),
+        in_=raw_codes[:].rearrange("p a b -> p (a b)").bitcast(I32).rearrange("p (q m) -> p m q", m=O_TILES),
+    )
+    w_scales = pool.tile([P, O_TILES, O_TILE], U8, align_bytes=64)
+    nc.vector.tensor_copy(
+        out=w_scales[:],
+        in_=raw_scales[:].rearrange("p a b -> p (a b)").rearrange("p (q m) -> p m q", m=O_TILES),
     )
     return w_codes, w_scales
 
@@ -54,18 +69,19 @@ def tile_simpleconvolution_kernel(tc, x, weight_words, weight_scales, out):
         weight_pool = ctx.enter_context(tc.tile_pool(name="weight", bufs=1))
         image_pool = ctx.enter_context(tc.tile_pool(name="image", bufs=IMAGES))
         unit_pool = ctx.enter_context(tc.tile_pool(name="unit", bufs=UNITS))
-        result_pool = ctx.enter_context(tc.tile_pool(name="result", bufs=9))
+        result_pool = ctx.enter_context(tc.tile_pool(name="result", bufs=12))
         psum = ctx.enter_context(tc.psum_pool(name="psum", bufs=PSUM_BANKS))
         ctx.enter_context(tc.manual_schedule())
 
         raws = [load_image(nc, image_pool, x, 0)]
-        w_codes, w_scales = load_weight(nc, weight_pool, weight_words, weight_scales)
+        raw_codes, raw_scales = load_weight(nc, weight_pool, weight_words, weight_scales)
         for b in range(1, IMAGES):
             raws.append(load_image(nc, image_pool, x, b))
 
         grouped = {}
         x_codes = {}
         x_scales = {}
+        weights = {False: (raw_codes, raw_scales)}
 
         def regroup(u, engine_copy):
             b, n = divmod(u, HALVES)
@@ -88,13 +104,13 @@ def tile_simpleconvolution_kernel(tc, x, weight_words, weight_scales, out):
             x_codes[u] = codes
             x_scales[u] = scales
 
-        def multiply(u, m):
-            o_cols = slice(m * O_TILE, (m + 1) * O_TILE)
+        def multiply(u, m, permuted):
+            w_codes, w_scales = weights[permuted]
             acc = psum.tile([P, PX_TILE], F32, name="acc")
             nc.tensor.matmul_mx(
                 out=acc[:],
-                lhsT=w_codes[:, o_cols].bitcast(FP8X4),
-                lhsT_scale=w_scales[:, o_cols],
+                lhsT=w_codes[:, m, :].bitcast(FP8X4),
+                lhsT_scale=w_scales[:, m, :],
                 rhs=x_codes[u][:].bitcast(FP8X4),
                 rhs_scale=x_scales[u][:],
                 start=True,
@@ -104,8 +120,8 @@ def tile_simpleconvolution_kernel(tc, x, weight_words, weight_scales, out):
 
         on_vector = nc.vector.tensor_copy
         on_scalar = nc.scalar.copy
-        vector_tiles = ((), (0,), (0,), (0, 2))
-        store_groups = (((0,), (1,), (2, 3)), ((0, 1), (2, 3)), ((0, 1), (2, 3)), ((0, 1), (2, 3)))
+        vector_tiles = ((), (0,), (), (0, 1, 3))
+        store_groups = (((0,), (1,), (2,), (3,)), ((0, 1), (2, 3)), ((0,), (1,), (2,), (3,)), ((0, 1), (2, 3)))
 
         for b in range(IMAGES):
             units = [HALVES * b + n for n in range(HALVES)]
@@ -113,12 +129,18 @@ def tile_simpleconvolution_kernel(tc, x, weight_words, weight_scales, out):
             regroup(units[1], on_scalar if b == 0 else on_vector)
             for u in units:
                 quantise(u)
-            out_b = out[b].rearrange("(m p) h w -> p m (h w)", p=O_TILE)
+            if b == 0:
+                weights[True] = permute_weight(nc, weight_pool, raw_codes, raw_scales)
+            permuted = len(store_groups[b]) < O_TILES
+            if permuted:
+                out_b = out[b].rearrange("(q m) h w -> q m (h w)", m=O_TILES)
+            else:
+                out_b = out[b].rearrange("(m p) h w -> p m (h w)", p=O_TILE)
             for group in store_groups[b]:
                 result = result_pool.tile([P, len(group), PIXELS], F32, name="result")
                 for i, m in enumerate(group):
                     engine_copy = on_vector if m in vector_tiles[b] else on_scalar
                     for n, u in enumerate(units):
-                        acc = multiply(u, m)
+                        acc = multiply(u, m, permuted)
                         engine_copy(out=result[:, i, n * PX_TILE : (n + 1) * PX_TILE], in_=acc[:])
                 nc.sync.dma_start(out=out_b[:, group[0] : group[-1] + 1, :], in_=result[:])

@@ -26,10 +26,13 @@ RUN = 4
 FLOPS = 2 * IMAGES * PIXELS * C_IN * C_OUT
 
 
-def load_image(nc, pool, x, b):
-    raw = pool.tile([P, PACK, PIXELS], BF16)
-    nc.sync.dma_start(out=raw[:], in_=x[b].rearrange("(p j) h w -> p j (h w)", j=PACK))
-    return raw
+def load_images(nc, pool, x, first, count):
+    raw = pool.tile([P, count, PACK, PIXELS], BF16, name="raw%d" % first)
+    nc.sync.dma_start(
+        out=raw[:].rearrange("p b j x -> p b (j x)"),
+        in_=x[first : first + count].rearrange("b (p j) h w -> p b (j h w)", j=PACK),
+    )
+    return [raw[:, i] for i in range(count)]
 
 
 def load_weight(nc, pool, weight_words, weight_scales):
@@ -49,34 +52,38 @@ def load_weight(nc, pool, weight_words, weight_scales):
     return raw_codes, raw_scales
 
 
-def permute_weight(nc, pool, raw_codes, raw_scales):
+def permute_codes(nc, pool, raw_codes):
     w_codes = pool.tile([P, O_TILES, O_TILE], U32, align_bytes=64)
     nc.vector.tensor_copy(
         out=w_codes[:].bitcast(I32),
         in_=raw_codes[:].rearrange("p a b -> p (a b)").bitcast(I32).rearrange("p (q m) -> p m q", m=O_TILES),
     )
+    return w_codes
+
+
+def permute_scales(nc, pool, raw_scales):
     w_scales = pool.tile([P, O_TILES, O_TILE], U8, align_bytes=64)
     nc.vector.tensor_copy(
         out=w_scales[:],
         in_=raw_scales[:].rearrange("p a b -> p (a b)").rearrange("p (q m) -> p m q", m=O_TILES),
     )
-    return w_codes, w_scales
+    return w_scales
 
 
 def tile_simpleconvolution_kernel(tc, x, weight_words, weight_scales, out):
     nc = tc.nc
     with ExitStack() as ctx:
         weight_pool = ctx.enter_context(tc.tile_pool(name="weight", bufs=1))
-        image_pool = ctx.enter_context(tc.tile_pool(name="image", bufs=IMAGES))
+        image_pool = ctx.enter_context(tc.tile_pool(name="image", bufs=1))
         unit_pool = ctx.enter_context(tc.tile_pool(name="unit", bufs=UNITS))
         result_pool = ctx.enter_context(tc.tile_pool(name="result", bufs=12))
         psum = ctx.enter_context(tc.psum_pool(name="psum", bufs=PSUM_BANKS))
         ctx.enter_context(tc.manual_schedule())
 
-        raws = [load_image(nc, image_pool, x, 0)]
+        raws = load_images(nc, image_pool, x, 0, 1)
         raw_codes, raw_scales = load_weight(nc, weight_pool, weight_words, weight_scales)
-        for b in range(1, IMAGES):
-            raws.append(load_image(nc, image_pool, x, b))
+        raws.extend(load_images(nc, image_pool, x, 1, 1))
+        raws.extend(load_images(nc, image_pool, x, 2, 2))
 
         grouped = {}
         x_codes = {}
@@ -126,11 +133,13 @@ def tile_simpleconvolution_kernel(tc, x, weight_words, weight_scales, out):
         for b in range(IMAGES):
             units = [HALVES * b + n for n in range(HALVES)]
             regroup(units[0], on_vector)
+            if b == 0:
+                w_codes = permute_codes(nc, weight_pool, raw_codes)
             regroup(units[1], on_scalar if b == 0 else on_vector)
             for u in units:
                 quantise(u)
             if b == 0:
-                weights[True] = permute_weight(nc, weight_pool, raw_codes, raw_scales)
+                weights[True] = (w_codes, permute_scales(nc, weight_pool, raw_scales))
             permuted = len(store_groups[b]) < O_TILES
             if permuted:
                 out_b = out[b].rearrange("(q m) h w -> q m (h w)", m=O_TILES)

@@ -22,6 +22,7 @@ HALVES = PIXELS // PX_TILE
 UNITS = IMAGES * HALVES
 PSUM_BANKS = 8
 RUN = 4
+WARM_PASSES = 4
 
 FLOPS = 2 * IMAGES * PIXELS * C_IN * C_OUT
 
@@ -85,6 +86,12 @@ def tile_simpleconvolution_kernel(tc, x, weight_words, weight_scales, out):
         raws.extend(load_images(nc, image_pool, x, 1, 1))
         raws.extend(load_images(nc, image_pool, x, 2, 2))
 
+        warm = psum.tile([P, PX_TILE], F32, name="acc")
+        for i in range(WARM_PASSES):
+            nc.tensor.matmul(
+                out=warm[:], lhsT=raws[0][:, 0, 0:P], rhs=raws[0][:, 0, 0:PX_TILE], start=True, stop=True
+            )
+
         grouped = {}
         x_codes = {}
         x_scales = {}
@@ -134,12 +141,13 @@ def tile_simpleconvolution_kernel(tc, x, weight_words, weight_scales, out):
             units = [HALVES * b + n for n in range(HALVES)]
             regroup(units[0], on_vector)
             if b == 0:
-                w_codes = permute_codes(nc, weight_pool, raw_codes)
+                weights[True] = (
+                    permute_codes(nc, weight_pool, raw_codes),
+                    permute_scales(nc, weight_pool, raw_scales),
+                )
             regroup(units[1], on_scalar if b == 0 else on_vector)
             for u in units:
                 quantise(u)
-            if b == 0:
-                weights[True] = (w_codes, permute_scales(nc, weight_pool, raw_scales))
             permuted = len(store_groups[b]) < O_TILES
             if permuted:
                 out_b = out[b].rearrange("(q m) h w -> q m (h w)", m=O_TILES)

@@ -22,6 +22,7 @@ HALVES = PIXELS // PX_TILE
 UNITS = IMAGES * HALVES
 PSUM_BANKS = 8
 RUN = 4
+VECTOR_SHARE = 128
 WARM_PASSES = 4
 
 FLOPS = 2 * IMAGES * PIXELS * C_IN * C_OUT
@@ -77,7 +78,7 @@ def tile_simpleconvolution_kernel(tc, x, weight_words, weight_scales, out):
         weight_pool = ctx.enter_context(tc.tile_pool(name="weight", bufs=1))
         image_pool = ctx.enter_context(tc.tile_pool(name="image", bufs=1))
         unit_pool = ctx.enter_context(tc.tile_pool(name="unit", bufs=UNITS))
-        result_pool = ctx.enter_context(tc.tile_pool(name="result", bufs=12))
+        result_pool = ctx.enter_context(tc.tile_pool(name="result", bufs=IMAGES))
         psum = ctx.enter_context(tc.psum_pool(name="psum", bufs=PSUM_BANKS))
         ctx.enter_context(tc.manual_schedule())
 
@@ -92,20 +93,22 @@ def tile_simpleconvolution_kernel(tc, x, weight_words, weight_scales, out):
                 out=warm[:], lhsT=raws[0][:, 0, 0:P], rhs=raws[0][:, 0, 0:PX_TILE], start=True, stop=True
             )
 
-        grouped = {}
         x_codes = {}
         x_scales = {}
-        weights = {False: (raw_codes, raw_scales)}
+        grouped = {}
+        on_vector = nc.vector.tensor_copy
+        on_scalar = nc.scalar.copy
 
-        def regroup(u, engine_copy):
+        def new_unit(u):
+            grouped[u] = unit_pool.tile([P, PX_TILE, PACK], BF16, align_bytes=64, name="grouped")
+
+        def regroup(u, engine_copy, first=0, last=PX_TILE):
             b, n = divmod(u, HALVES)
-            px = slice(n * PX_TILE, (n + 1) * PX_TILE)
-            g = unit_pool.tile([P, PX_TILE, PACK], BF16, align_bytes=64, name="grouped")
+            px = slice(n * PX_TILE + first, n * PX_TILE + last)
             engine_copy(
-                out=g[:].rearrange("p (c i) j -> p c j i", i=RUN),
+                out=grouped[u][:, first:last, :].rearrange("p (c i) j -> p c j i", i=RUN),
                 in_=raws[b][:, :, px].rearrange("p j (c i) -> p c j i", i=RUN),
             )
-            grouped[u] = g
 
         def quantise(u):
             codes = unit_pool.tile([P, PX_TILE], U32, align_bytes=64, name="codes")
@@ -118,8 +121,8 @@ def tile_simpleconvolution_kernel(tc, x, weight_words, weight_scales, out):
             x_codes[u] = codes
             x_scales[u] = scales
 
-        def multiply(u, m, permuted):
-            w_codes, w_scales = weights[permuted]
+        def multiply(u, m, weights):
+            w_codes, w_scales = weights
             acc = psum.tile([P, PX_TILE], F32, name="acc")
             nc.tensor.matmul_mx(
                 out=acc[:],
@@ -132,32 +135,50 @@ def tile_simpleconvolution_kernel(tc, x, weight_words, weight_scales, out):
             )
             return acc
 
-        on_vector = nc.vector.tensor_copy
-        on_scalar = nc.scalar.copy
-        vector_tiles = ((), (0,), (), (0, 1, 3))
-        store_groups = (((0,), (1,), (2,), (3,)), ((0, 1), (2, 3)), ((0,), (1,), (2,), (3,)), ((0, 1), (2, 3)))
+        vector_banks = {(1, 1, 0), (2, 3, 1), (3, 1, 1), (3, 2, 1), (3, 3, 1)}
+        store_groups = (((0, 1), (1, 2), (2, 4)), ((0, 2), (2, 4)), ((0, 2), (2, 4)), ((0, 4),))
+        permuted = []
 
-        for b in range(IMAGES):
-            units = [HALVES * b + n for n in range(HALVES)]
-            regroup(units[0], on_vector)
-            if b == 0:
-                weights[True] = (
-                    permute_codes(nc, weight_pool, raw_codes),
-                    permute_scales(nc, weight_pool, raw_scales),
-                )
-            regroup(units[1], on_scalar if b == 0 else on_vector)
-            for u in units:
-                quantise(u)
-            permuted = len(store_groups[b]) < O_TILES
-            if permuted:
+        def products(b):
+            weights = permuted if b > 0 else (raw_codes, raw_scales)
+            if b > 0:
                 out_b = out[b].rearrange("(q m) h w -> q m (h w)", m=O_TILES)
             else:
                 out_b = out[b].rearrange("(m p) h w -> p m (h w)", p=O_TILE)
-            for group in store_groups[b]:
-                result = result_pool.tile([P, len(group), PIXELS], F32, name="result")
-                for i, m in enumerate(group):
-                    engine_copy = on_vector if m in vector_tiles[b] else on_scalar
-                    for n, u in enumerate(units):
-                        acc = multiply(u, m, permuted)
-                        engine_copy(out=result[:, i, n * PX_TILE : (n + 1) * PX_TILE], in_=acc[:])
-                nc.sync.dma_start(out=out_b[:, group[0] : group[-1] + 1, :], in_=result[:])
+            result = result_pool.tile([P, O_TILES, PIXELS], F32, name="result")
+            banks = [(m, n) for m in range(O_TILES) for n in range(HALVES)]
+            if b == IMAGES - 1:
+                banks = [(m, n) for n in range(HALVES) for m in range(O_TILES)]
+            for m, n in banks:
+                acc = multiply(HALVES * b + n, m, weights)
+                engine_copy = on_vector if (b, m, n) in vector_banks else on_scalar
+                engine_copy(out=result[:, m, n * PX_TILE : (n + 1) * PX_TILE], in_=acc[:])
+            for first, last in store_groups[b]:
+                nc.sync.dma_start(out=out_b[:, first:last, :], in_=result[:, first:last, :])
+
+        for u in range(UNITS):
+            new_unit(u)
+
+        regroup(0, on_vector)
+        regroup(1, on_scalar, VECTOR_SHARE, PX_TILE)
+        regroup(1, on_vector, 0, VECTOR_SHARE)
+        quantise(0)
+        quantise(1)
+        permuted.append(permute_codes(nc, weight_pool, raw_codes))
+        permuted.append(permute_scales(nc, weight_pool, raw_scales))
+        products(0)
+        regroup(2, on_vector)
+        regroup(3, on_vector)
+        quantise(2)
+        quantise(3)
+        regroup(4, on_vector)
+        products(1)
+        regroup(5, on_vector)
+        quantise(4)
+        quantise(5)
+        regroup(6, on_vector)
+        regroup(7, on_vector)
+        quantise(6)
+        quantise(7)
+        products(2)
+        products(3)

@@ -22,7 +22,6 @@ HALVES = PIXELS // PX_TILE
 UNITS = IMAGES * HALVES
 PSUM_BANKS = 8
 RUN = 4
-VECTOR_SHARE = 128
 WARM_PASSES = 4
 
 FLOPS = 2 * IMAGES * PIXELS * C_IN * C_OUT
@@ -135,8 +134,8 @@ def tile_simpleconvolution_kernel(tc, x, weight_words, weight_scales, out):
             )
             return acc
 
-        vector_banks = {(1, 1, 0), (2, 3, 1), (3, 1, 1), (3, 2, 1), (3, 3, 1)}
-        store_groups = (((0, 1), (1, 2), (2, 4)), ((0, 2), (2, 4)), ((0, 2), (2, 4)), ((0, 4),))
+        vector_banks = {(1, 1, 0), (2, 3, 1), (3, 0, 0), (3, 1, 0), (3, 0, 1), (3, 1, 1)}
+        store_groups = (((0, 2), (2, 4)), ((0, 2), (2, 4)), ((0, 2), (2, 4)), ((0, 4),))
         permuted = []
 
         def products(b):
@@ -146,26 +145,22 @@ def tile_simpleconvolution_kernel(tc, x, weight_words, weight_scales, out):
             else:
                 out_b = out[b].rearrange("(m p) h w -> p m (h w)", p=O_TILE)
             result = result_pool.tile([P, O_TILES, PIXELS], F32, name="result")
-            banks = [(m, n) for m in range(O_TILES) for n in range(HALVES)]
-            if b == IMAGES - 1:
-                banks = [(m, n) for n in range(HALVES) for m in range(O_TILES)]
-            for m, n in banks:
-                acc = multiply(HALVES * b + n, m, weights)
-                engine_copy = on_vector if (b, m, n) in vector_banks else on_scalar
-                engine_copy(out=result[:, m, n * PX_TILE : (n + 1) * PX_TILE], in_=acc[:])
             for first, last in store_groups[b]:
+                for m, n in [(m, n) for n in range(HALVES) for m in range(first, last)]:
+                    acc = multiply(HALVES * b + n, m, weights)
+                    engine_copy = on_vector if (b, m, n) in vector_banks else on_scalar
+                    engine_copy(out=result[:, m, n * PX_TILE : (n + 1) * PX_TILE], in_=acc[:])
                 nc.sync.dma_start(out=out_b[:, first:last, :], in_=result[:, first:last, :])
 
         for u in range(UNITS):
             new_unit(u)
 
         regroup(0, on_vector)
-        regroup(1, on_scalar, VECTOR_SHARE, PX_TILE)
-        regroup(1, on_vector, 0, VECTOR_SHARE)
-        quantise(0)
-        quantise(1)
+        regroup(1, on_scalar)
         permuted.append(permute_codes(nc, weight_pool, raw_codes))
+        quantise(0)
         permuted.append(permute_scales(nc, weight_pool, raw_scales))
+        quantise(1)
         products(0)
         regroup(2, on_vector)
         regroup(3, on_vector)

@@ -22,6 +22,7 @@ HALVES = PIXELS // PX_TILE
 UNITS = IMAGES * HALVES
 PSUM_BANKS = 8
 RUN = 4
+VECTOR_SHARE = 128
 WARM_PASSES = 4
 
 FLOPS = 2 * IMAGES * PIXELS * C_IN * C_OUT
@@ -135,7 +136,7 @@ def tile_simpleconvolution_kernel(tc, x, weight_words, weight_scales, out):
             return acc
 
         vector_banks = {(1, 1, 0), (2, 3, 1), (3, 0, 0), (3, 1, 0), (3, 0, 1), (3, 1, 1)}
-        store_groups = (((0, 2), (2, 4)), ((0, 2), (2, 4)), ((0, 2), (2, 4)), ((0, 4),))
+        store_groups = (((0, 1), (1, 2), (2, 4)), ((0, 2), (2, 4)), ((0, 2), (2, 4)), ((0, 4),))
         permuted = []
 
         def products(b):
@@ -156,11 +157,12 @@ def tile_simpleconvolution_kernel(tc, x, weight_words, weight_scales, out):
             new_unit(u)
 
         regroup(0, on_vector)
-        regroup(1, on_scalar)
-        permuted.append(permute_codes(nc, weight_pool, raw_codes))
+        regroup(1, on_scalar, VECTOR_SHARE, PX_TILE)
+        regroup(1, on_vector, 0, VECTOR_SHARE)
         quantise(0)
-        permuted.append(permute_scales(nc, weight_pool, raw_scales))
         quantise(1)
+        permuted.append(permute_codes(nc, weight_pool, raw_codes))
+        permuted.append(permute_scales(nc, weight_pool, raw_scales))
         products(0)
         regroup(2, on_vector)
         regroup(3, on_vector)

from contextlib import ExitStack

import concourse.mybir as mybir

FP8X4 = mybir.dt.float8_e4m3fn_x4
BF16 = mybir.dt.bfloat16
F32 = mybir.dt.float32
I32 = mybir.dt.int32
U32 = mybir.dt.uint32
U8 = mybir.dt.uint8

P = 128
PACK = 4
IMAGES = 4
C_IN = P * PACK
C_OUT = 512
PIXELS = 32 * 32
O_TILE = 128
PX_TILE = 512
O_TILES = C_OUT // O_TILE
HALVES = PIXELS // PX_TILE
UNITS = IMAGES * HALVES
PSUM_BANKS = 8
RUN = 4
VECTOR_SHARE = 128
WARM_PASSES = 4

FLOPS = 2 * IMAGES * PIXELS * C_IN * C_OUT


def load_images(nc, pool, x, first, count):
    raw = pool.tile([P, count, PACK, PIXELS], BF16, name="raw%d" % first)
    nc.sync.dma_start(
        out=raw[:].rearrange("p b j x -> p b (j x)"),
        in_=x[first : first + count].rearrange("b (p j) h w -> p b (j h w)", j=PACK),
    )
    return [raw[:, i] for i in range(count)]


def load_weight(nc, pool, weight_words, weight_scales):
    raw_scales = pool.tile([P, O_TILES, O_TILE], U8, align_bytes=64)
    flat_scales = raw_scales[:].rearrange("p m q -> p (m q)")
    nc.vector.memset(flat_scales.bitcast(I32), 0)
    for quadrant in range(4):
        nc.sync.dma_start(
            out=flat_scales[32 * quadrant : 32 * quadrant + 4, :].bitcast(I32),
            in_=weight_scales[0, 4 * quadrant : 4 * quadrant + 4, :].bitcast(I32),
        )
    raw_codes = pool.tile([P, O_TILES, O_TILE], U32, align_bytes=64)
    nc.sync.dma_start(
        out=raw_codes[:].rearrange("p m q -> p (m q)").bitcast(I32),
        in_=weight_words[0].rearrange("p n t -> p (n t)").bitcast(I32),
    )
    return raw_codes, raw_scales


def permute_codes(nc, pool, raw_codes):
    w_codes = pool.tile([P, O_TILES, O_TILE], U32, align_bytes=64)
    nc.vector.tensor_copy(
        out=w_codes[:].bitcast(I32),
        in_=raw_codes[:].rearrange("p a b -> p (a b)").bitcast(I32).rearrange("p (q m) -> p m q", m=O_TILES),
    )
    return w_codes


def permute_scales(nc, pool, raw_scales):
    w_scales = pool.tile([P, O_TILES, O_TILE], U8, align_bytes=64)
    nc.vector.tensor_copy(
        out=w_scales[:],
        in_=raw_scales[:].rearrange("p a b -> p (a b)").rearrange("p (q m) -> p m q", m=O_TILES),
    )
    return w_scales


def tile_simpleconvolution_kernel(tc, x, weight_words, weight_scales, out):
    nc = tc.nc
    with ExitStack() as ctx:
        weight_pool = ctx.enter_context(tc.tile_pool(name="weight", bufs=1))
        image_pool = ctx.enter_context(tc.tile_pool(name="image", bufs=1))
        unit_pool = ctx.enter_context(tc.tile_pool(name="unit", bufs=UNITS))
        result_pool = ctx.enter_context(tc.tile_pool(name="result", bufs=IMAGES))
        psum = ctx.enter_context(tc.psum_pool(name="psum", bufs=PSUM_BANKS))
        ctx.enter_context(tc.manual_schedule())

        raws = load_images(nc, image_pool, x, 0, 1)
        raw_codes, raw_scales = load_weight(nc, weight_pool, weight_words, weight_scales)
        raws.extend(load_images(nc, image_pool, x, 1, 1))
        raws.extend(load_images(nc, image_pool, x, 2, 2))

        warm = psum.tile([P, PX_TILE], F32, name="acc")
        for i in range(WARM_PASSES):
            nc.tensor.matmul(
                out=warm[:], lhsT=raws[0][:, 0, 0:P], rhs=raws[0][:, 0, 0:PX_TILE], start=True, stop=True
            )

        x_codes = {}
        x_scales = {}
        grouped = {}
        on_vector = nc.vector.tensor_copy
        on_scalar = nc.scalar.copy

        def new_unit(u):
            grouped[u] = unit_pool.tile([P, PX_TILE, PACK], BF16, align_bytes=64, name="grouped")

        def regroup(u, engine_copy, first=0, last=PX_TILE):
            b, n = divmod(u, HALVES)
            px = slice(n * PX_TILE + first, n * PX_TILE + last)
            engine_copy(
                out=grouped[u][:, first:last, :].rearrange("p (c i) j -> p c j i", i=RUN),
                in_=raws[b][:, :, px].rearrange("p j (c i) -> p c j i", i=RUN),
            )

        def quantise(u):
            codes = unit_pool.tile([P, PX_TILE], U32, align_bytes=64, name="codes")
            scales = unit_pool.tile([P, PX_TILE], U8, align_bytes=64, name="scales")
            nc.vector.quantize_mx(
                out=codes[:].bitcast(FP8X4),
                scales=scales[:],
                in_=grouped[u][:].rearrange("p w j -> p (w j)"),
            )
            x_codes[u] = codes
            x_scales[u] = scales

        def multiply(u, m, weights):
            w_codes, w_scales = weights
            acc = psum.tile([P, PX_TILE], F32, name="acc")
            nc.tensor.matmul_mx(
                out=acc[:],
                lhsT=w_codes[:, m, :].bitcast(FP8X4),
                lhsT_scale=w_scales[:, m, :],
                rhs=x_codes[u][:].bitcast(FP8X4),
                rhs_scale=x_scales[u][:],
                start=True,
                stop=True,
            )
            return acc

        vector_banks = {(1, 1, 0), (2, 3, 1), (3, 0, 0), (3, 1, 0), (3, 0, 1), (3, 1, 1)}
        store_groups = (((0, 1), (1, 2), (2, 4)), ((0, 2), (2, 4)), ((0, 2), (2, 4)), ((0, 4),))
        permuted = []

        def products(b):
            weights = permuted if b > 0 else (raw_codes, raw_scales)
            if b > 0:
                out_b = out[b].rearrange("(q m) h w -> q m (h w)", m=O_TILES)
            else:
                out_b = out[b].rearrange("(m p) h w -> p m (h w)", p=O_TILE)
            result = result_pool.tile([P, O_TILES, PIXELS], F32, name="result")
            for first, last in store_groups[b]:
                for m, n in [(m, n) for n in range(HALVES) for m in range(first, last)]:
                    acc = multiply(HALVES * b + n, m, weights)
                    engine_copy = on_vector if (b, m, n) in vector_banks else on_scalar
                    engine_copy(out=result[:, m, n * PX_TILE : (n + 1) * PX_TILE], in_=acc[:])
                nc.sync.dma_start(out=out_b[:, first:last, :], in_=result[:, first:last, :])

        for u in range(UNITS):
            new_unit(u)

        regroup(0, on_vector)
        regroup(1, on_scalar, VECTOR_SHARE, PX_TILE)
        regroup(1, on_vector, 0, VECTOR_SHARE)
        quantise(0)
        quantise(1)
        permuted.append(permute_codes(nc, weight_pool, raw_codes))
        permuted.append(permute_scales(nc, weight_pool, raw_scales))
        products(0)
        regroup(2, on_vector)
        regroup(3, on_vector)
        quantise(2)
        quantise(3)
        regroup(4, on_vector)
        products(1)
        regroup(5, on_vector)
        quantise(4)
        quantise(5)
        regroup(6, on_vector)
        regroup(7, on_vector)
        quantise(6)
        quantise(7)
        products(2)
        products(3)
